import numpy as np
import ml_dtypes


def mxq(x, axis, fmt="e4m3"):
    dtype, down = {"e4m3": (ml_dtypes.float8_e4m3fn, 7), "e5m2": (ml_dtypes.float8_e5m2, 14)}[fmt]
    v = np.moveaxis(np.asarray(x, np.float32).astype(ml_dtypes.bfloat16).astype(np.float64), axis, -1)
    blocks = v.reshape(v.shape[:-1] + (-1, 32))
    amax = np.abs(blocks).max(-1, keepdims=True)
    byte = np.maximum(np.where(amax > 0, np.frexp(amax)[1] - 1 + 127, 0) - down, 1)
    scale = np.exp2(byte - 127.0)
    codes = (blocks / scale).astype(np.float32).astype(dtype).astype(np.float64)
    return np.moveaxis((codes * scale).reshape(v.shape), -1, axis)


WIDE = False


def mx_kscale(k):
    if not WIDE:
        return np.ones(k)
    levels = np.array([10, -10, 5, -5, 0])
    if k % 512:
        return np.exp2(np.random.permutation(np.resize(levels, k // 32))).repeat(32)
    a = np.empty((k // 512, 16))
    for p in range(k // 512):
        a[p, :8] = np.random.permutation(np.resize(levels, 8))
        for g in range(8):
            far = levels[np.abs(levels - a[p, g]) >= 10]
            a[p, g + 8] = far[np.random.randint(len(far))]
    return np.exp2(a.ravel()).repeat(32)


BF16 = ml_dtypes.bfloat16


def bf(x):
    return np.asarray(x, np.float32).astype(BF16)


def f64(x):
    return np.asarray(x).astype(np.float64)


N, K, C = 1024, 256, 512


def draw(rows, f, total):
    x = np.random.standard_normal((rows, f.size))
    for v in np.unique(f):
        m = f == v
        x[:, m] -= x[:, m].mean(1, keepdims=True)
    top = (f == f.max()).astype(np.float64)
    return np.sqrt(K / (2.0 * np.sqrt(C))) * x * f + total * np.random.standard_normal((rows, 1)) * top / top.sum()


def setup_inputs():
    s = mx_kscale(C)
    return {"output": bf(draw(N, s, 0.3 * K)), "code_book": bf(draw(K, 1.0 / s, 0.3 * K))}


def reference(output, code_book):
    output, code_book = f64(output), f64(code_book)
    K, C = code_book.shape
    dot = mxq(output, 1, "e4m3") @ mxq(code_book, 1, "e4m3").T
    o_sum = np.sum(output, axis=1, keepdims=True)
    c_sum = np.sum(code_book, axis=1)[None, :]
    return (2.0 * dot + float(C) - o_sum - c_sum) / float(K)

@@ -1,0 +1,158 @@
+from contextlib import ExitStack
+
+import concourse.mybir as mybir
+from concourse.masks import make_identity
+
+F32 = mybir.dt.float32
+BF16 = mybir.dt.bfloat16
+U32 = mybir.dt.uint32
+U8 = mybir.dt.uint8
+FP8X4 = mybir.dt.float8_e4m3fn_x4
+ALU = mybir.AluOpType
+FUNC = mybir.ActivationFunctionType
+
+P = 128
+ROWS = 1024
+CODES = 256
+LENGTH = 512
+WORDS = LENGTH // 2
+ROW_TILES = ROWS // P
+CODE_TILES = CODES // P
+PAIR = 2
+CHUNKS = ROW_TILES // PAIR
+
+FLOPS = 2 * ROWS * CODES * LENGTH
+
+
+def sum_rows_vector(nc, rows, scratch, total):
+    nc.vector.tensor_scalar(
+        out=scratch,
+        in0=rows,
+        scalar1=-1.0 / CODES,
+        scalar2=None,
+        op0=ALU.mult,
+        op1=ALU.add,
+        accum_out=total,
+    )
+
+
+def sum_rows_scalar(nc, rows, scratch, total):
+    nc.scalar.activation(out=scratch, in_=rows, func=FUNC.Identity, scale=-1.0 / CODES, accum_out=total)
+
+
+def tile_codingclassifier_s_kernel(tc, output, code_book, out):
+    nc = tc.nc
+    x_view = output.rearrange("(p r) c -> p r c", r=ROW_TILES)
+    out_view = out.rearrange("(p r) k -> p r k", r=ROW_TILES)
+
+    with ExitStack() as ctx:
+        ctx.enter_context(tc.manual_schedule())
+        keep = ctx.enter_context(tc.tile_pool(name="keep", bufs=1))
+        work = ctx.enter_context(tc.tile_pool(name="work", bufs=CHUNKS))
+        t_psum = ctx.enter_context(tc.psum_pool(name="t_psum", bufs=4))
+        dot_psum = ctx.enter_context(tc.psum_pool(name="dot_psum", bufs=3))
+        c_psum = ctx.enter_context(tc.psum_pool(name="c_psum", bufs=1))
+
+        y_rows = keep.tile([P, PAIR, LENGTH], BF16)
+        nc.sync.dma_start(out=y_rows[:], in_=code_book.rearrange("(a p) c -> p a c", p=P))
+        pairs = [y_rows]
+        for chunk in range(CHUNKS):
+            x_rows = work.tile([P, PAIR, LENGTH], BF16)
+            nc.sync.dma_start(out=x_rows[:], in_=x_view[:, chunk * PAIR : (chunk + 1) * PAIR, :])
+            pairs.append(x_rows)
+
+        identity = keep.tile([P, P], F32)
+        make_identity(nc, identity[:])
+
+        warm = keep.tile([P, 1], F32)
+        nc.vector.memset(warm[:], 0.0)
+        warmed = keep.tile([P, 1], F32)
+        nc.scalar.activation(out=warmed[:], in_=warm[:], func=FUNC.Identity)
+
+        scratch = keep.tile([P, 1 + CHUNKS, PAIR, LENGTH], BF16)
+        c_part_a = keep.tile([P, 1], F32)
+        c_part_b = keep.tile([P, 1], F32)
+        o_term = keep.tile([P, ROW_TILES], F32)
+        c_term = keep.tile([P, CODES], F32)
+
+        grouped = keep.tile([P, 1 + CHUNKS, PAIR * P * 4], BF16, align_bytes=64)
+        codes = keep.tile([P, 1 + CHUNKS, PAIR * P], U32, align_bytes=64)
+        scales = keep.tile([P, 1 + CHUNKS, PAIR * P], U8, align_bytes=64)
+        both_terms = keep.tile([P, CHUNKS, PAIR * CODES], F32)
+
+        def sums(i):
+            if i == 0:
+                sum_rows_scalar(nc, y_rows[:, 0, :], scratch[:, 0, 0, :], c_part_a[:])
+                sum_rows_vector(nc, y_rows[:, 1, :], scratch[:, 0, 1, :], c_part_b[:])
+            else:
+                for j in range(PAIR):
+                    r = (i - 1) * PAIR + j
+                    sum_rows_vector(nc, pairs[i][:, j, :], scratch[:, i, j, :], o_term[:, r : r + 1])
+
+        def transpose(i):
+            words = pairs[i][:].bitcast(F32)
+            bank = t_psum.tile([P, PAIR, 2, P], F32)
+            for j in range(PAIR):
+                for u in range(2):
+                    nc.tensor.transpose(bank[:, j, u, :], words[:, j, u:WORDS:2], identity[:])
+            nc.scalar.copy(
+                out=grouped[:, i, :].bitcast(F32).rearrange("p (j n u) -> p j n u", j=PAIR, u=2),
+                in_=bank[:].rearrange("p j u n -> p j n u"),
+            )
+
+        def quantise(i):
+            nc.vector.quantize_mx(
+                out=codes[:, i, :].bitcast(FP8X4), scales=scales[:, i, :], in_=grouped[:, i, :]
+            )
+
+        def spread_c_term():
+            spread = c_psum.tile([P, CODES], F32)
+            nc.tensor.transpose(spread[:, 0:P], c_part_a[:].to_broadcast([P, P]), identity[:])
+            nc.tensor.transpose(spread[:, P:CODES], c_part_b[:].to_broadcast([P, P]), identity[:])
+            nc.scalar.activation(out=c_term[:], in_=spread[:], func=FUNC.Identity, bias=2.0, scale=1.0)
+
+        def add_terms(chunk):
+            for j in range(PAIR):
+                r = chunk * PAIR + j
+                nc.scalar.activation(
+                    out=both_terms[:, chunk, j * CODES : (j + 1) * CODES],
+                    in_=c_term[:],
+                    func=FUNC.Identity,
+                    bias=o_term[:, r : r + 1],
+                    scale=1.0,
+                )
+
+        for i in range(1 + CHUNKS + 1):
+            if i <= CHUNKS:
+                sums(i)
+                transpose(i)
+            if i >= 1:
+                quantise(i - 1)
+        spread_c_term()
+
+        for chunk in range(CHUNKS):
+            add_terms(chunk)
+            dot = dot_psum.tile([P, PAIR * CODES], F32)
+            for j in range(PAIR):
+                nc.tensor.matmul_mx(
+                    out=dot[:, j * CODES : (j + 1) * CODES],
+                    lhsT=codes[:, 1 + chunk, j * P : (j + 1) * P].bitcast(FP8X4),
+                    lhsT_scale=scales[:, 1 + chunk, j * P : (j + 1) * P],
+                    rhs=codes[:, 0, :].bitcast(FP8X4),
+                    rhs_scale=scales[:, 0, :],
+                    start=True,
+                    stop=True,
+                )
+            result = work.tile([P, PAIR * CODES], F32)
+            nc.vector.scalar_tensor_tensor(
+                out=result[:],
+                in0=dot[:],
+                scalar=2.0 / CODES,
+                in1=both_terms[:, chunk, :],
+                op0=ALU.mult,
+                op1=ALU.add,
+            )
+            nc.sync.dma_start(
+                out=out_view[:, chunk * PAIR : (chunk + 1) * PAIR, :],
+                in_=result[:].rearrange("p (j k) -> p j k", j=PAIR),
+            )

@@ -21,23 +21,20 @@ CODE_TILES = CODES // P
 PAIR = 2
 CHUNKS = ROW_TILES // PAIR
 
+Y_SCALE = 2.0 / CODES
+O_SCALE = -1.0 / CODES
+
 FLOPS = 2 * ROWS * CODES * LENGTH
 
 
-def sum_rows_vector(nc, rows, scratch, total):
+def scale_and_sum_vector(nc, rows, scaled, total, factor):
     nc.vector.tensor_scalar(
-        out=scratch,
-        in0=rows,
-        scalar1=-1.0 / CODES,
-        scalar2=None,
-        op0=ALU.mult,
-        op1=ALU.add,
-        accum_out=total,
+        out=scaled, in0=rows, scalar1=factor, scalar2=None, op0=ALU.mult, op1=ALU.add, accum_out=total
     )
 
 
-def sum_rows_scalar(nc, rows, scratch, total):
-    nc.scalar.activation(out=scratch, in_=rows, func=FUNC.Identity, scale=-1.0 / CODES, accum_out=total)
+def scale_and_sum_scalar(nc, rows, scaled, total, factor):
+    nc.scalar.activation(out=scaled, in_=rows, func=FUNC.Identity, scale=factor, accum_out=total)
 
 
 def tile_codingclassifier_s_kernel(tc, output, code_book, out):
@@ -50,16 +47,30 @@ def tile_codingclassifier_s_kernel(tc, output, code_book, out):
         keep = ctx.enter_context(tc.tile_pool(name="keep", bufs=1))
         work = ctx.enter_context(tc.tile_pool(name="work", bufs=CHUNKS))
         t_psum = ctx.enter_context(tc.psum_pool(name="t_psum", bufs=4))
-        dot_psum = ctx.enter_context(tc.psum_pool(name="dot_psum", bufs=3))
+        dot_psum = ctx.enter_context(tc.psum_pool(name="dot_psum", bufs=2))
         c_psum = ctx.enter_context(tc.psum_pool(name="c_psum", bufs=1))
+        o_psum = ctx.enter_context(tc.psum_pool(name="o_psum", bufs=1))
 
-        y_rows = keep.tile([P, PAIR, LENGTH], BF16)
-        nc.sync.dma_start(out=y_rows[:], in_=code_book.rearrange("(a p) c -> p a c", p=P))
-        pairs = [y_rows]
-        for chunk in range(CHUNKS):
-            x_rows = work.tile([P, PAIR, LENGTH], BF16)
-            nc.sync.dma_start(out=x_rows[:], in_=x_view[:, chunk * PAIR : (chunk + 1) * PAIR, :])
-            pairs.append(x_rows)
+        x_rows = []
+        y_rows = []
+
+        def load_x(chunk, pieces):
+            tiles = []
+            for piece in range(pieces):
+                span = PAIR // pieces
+                first = chunk * PAIR + piece * span
+                x_piece = keep.tile([P, span, LENGTH], BF16, name=f"x{chunk}_{piece}")
+                nc.sync.dma_start(out=x_piece[:], in_=x_view[:, first : first + span, :])
+                tiles.extend(x_piece[:, j, :] for j in range(span))
+            x_rows.append(tiles)
+
+        load_x(0, PAIR)
+        for a in range(CODE_TILES):
+            y_tile = keep.tile([P, LENGTH], BF16, name=f"y_tile{a}")
+            nc.sync.dma_start(out=y_tile[:], in_=code_book[a * P : (a + 1) * P, :])
+            y_rows.append(y_tile)
+        for chunk in range(1, CHUNKS):
+            load_x(chunk, 1)
 
         identity = keep.tile([P, P], F32)
         make_identity(nc, identity[:])
@@ -69,69 +80,65 @@ def tile_codingclassifier_s_kernel(tc, output, code_book, out):
         warmed = keep.tile([P, 1], F32)
         nc.scalar.activation(out=warmed[:], in_=warm[:], func=FUNC.Identity)
 
-        scratch = keep.tile([P, 1 + CHUNKS, PAIR, LENGTH], BF16)
-        c_part_a = keep.tile([P, 1], F32)
-        c_part_b = keep.tile([P, 1], F32)
-        o_term = keep.tile([P, ROW_TILES], F32)
+        y_scaled = [keep.tile([P, LENGTH], BF16, name=f"y_scaled{a}") for a in range(CODE_TILES)]
+        c_part = [keep.tile([P, 1], F32, name=f"c_part{a}") for a in range(CODE_TILES)]
+        o_scale = keep.tile([P, 1], BF16)
+        nc.vector.memset(o_scale[:], O_SCALE)
         c_term = keep.tile([P, CODES], F32)
+        scratch = [keep.tile([P, PAIR, LENGTH], BF16, name=f"scratch{i}") for i in range(CHUNKS)]
+        o_term = [keep.tile([P, PAIR], F32, name=f"o_term{i}") for i in range(CHUNKS)]
 
         grouped = keep.tile([P, 1 + CHUNKS, PAIR * P * 4], BF16, align_bytes=64)
         codes = keep.tile([P, 1 + CHUNKS, PAIR * P], U32, align_bytes=64)
         scales = keep.tile([P, 1 + CHUNKS, PAIR * P], U8, align_bytes=64)
-        both_terms = keep.tile([P, CHUNKS, PAIR * CODES], F32)
 
-        def sums(i):
-            if i == 0:
-                sum_rows_scalar(nc, y_rows[:, 0, :], scratch[:, 0, 0, :], c_part_a[:])
-                sum_rows_vector(nc, y_rows[:, 1, :], scratch[:, 0, 1, :], c_part_b[:])
-            else:
-                for j in range(PAIR):
-                    r = (i - 1) * PAIR + j
-                    sum_rows_vector(nc, pairs[i][:, j, :], scratch[:, i, j, :], o_term[:, r : r + 1])
-
-        def transpose(i):
-            words = pairs[i][:].bitcast(F32)
-            bank = t_psum.tile([P, PAIR, 2, P], F32)
-            for j in range(PAIR):
-                for u in range(2):
-                    nc.tensor.transpose(bank[:, j, u, :], words[:, j, u:WORDS:2], identity[:])
-            nc.scalar.copy(
-                out=grouped[:, i, :].bitcast(F32).rearrange("p (j n u) -> p j n u", j=PAIR, u=2),
-                in_=bank[:].rearrange("p j u n -> p j n u"),
-            )
+        def transpose(i, tiles, split):
+            packed = grouped[:, i, :].bitcast(F32).rearrange("p (j n u) -> p j n u", j=PAIR, u=2)
+            span = 1 if split else PAIR
+            for first in range(0, PAIR, span):
+                bank = t_psum.tile([P, PAIR, 2, P], F32)
+                for j in range(span):
+                    words = tiles[first + j].bitcast(F32)
+                    for u in range(2):
+                        nc.tensor.transpose(bank[:, j, u, :], words[:, u:WORDS:2], identity[:])
+                nc.scalar.copy(
+                    out=packed[:, first : first + span, :, :],
+                    in_=bank[:, 0:span, :, :].rearrange("p j u n -> p j n u"),
+                )
 
         def quantise(i):
             nc.vector.quantize_mx(
                 out=codes[:, i, :].bitcast(FP8X4), scales=scales[:, i, :], in_=grouped[:, i, :]
             )
 
-        def spread_c_term():
-            spread = c_psum.tile([P, CODES], F32)
-            nc.tensor.transpose(spread[:, 0:P], c_part_a[:].to_broadcast([P, P]), identity[:])
-            nc.tensor.transpose(spread[:, P:CODES], c_part_b[:].to_broadcast([P, P]), identity[:])
-            nc.scalar.activation(out=c_term[:], in_=spread[:], func=FUNC.Identity, bias=2.0, scale=1.0)
-
-        def add_terms(chunk):
-            for j in range(PAIR):
-                r = chunk * PAIR + j
-                nc.scalar.activation(
-                    out=both_terms[:, chunk, j * CODES : (j + 1) * CODES],
-                    in_=c_term[:],
-                    func=FUNC.Identity,
-                    bias=o_term[:, r : r + 1],
-                    scale=1.0,
+        def sums(chunk, scale_and_sum, tiles=range(PAIR)):
+            for j in tiles:
+                scale_and_sum(
+                    nc, x_rows[chunk][j], scratch[chunk][:, j, :], o_term[chunk][:, j : j + 1], O_SCALE
                 )
 
-        for i in range(1 + CHUNKS + 1):
-            if i <= CHUNKS:
-                sums(i)
-                transpose(i)
-            if i >= 1:
-                quantise(i - 1)
-        spread_c_term()
+        def sums_tensor(chunk):
+            total = o_psum.tile([P, PAIR], F32)
+            values = grouped[:, 1 + chunk, :].rearrange("p (j n t) -> p j n t", j=PAIR, t=4)
+            for j in range(PAIR):
+                for t in range(4):
+                    nc.tensor.matmul(
+                        total[:, j : j + 1], lhsT=values[:, j, :, t], rhs=o_scale[:], start=(t == 0), stop=(t == 3)
+                    )
+            o_term[chunk] = total
 
-        for chunk in range(CHUNKS):
-            add_terms(chunk)
+        def x_transpose(chunk, split=False):
+            transpose(1 + chunk, x_rows[chunk], split)
+
+        def spread_c_term():
+            spread = c_psum.tile([P, CODES], F32)
+            nc.tensor.transpose(spread[:, 0:P], c_part[0][:].to_broadcast([P, P]), identity[:])
+            nc.tensor.transpose(spread[:, P:CODES], c_part[1][:].to_broadcast([P, P]), identity[:])
+            nc.scalar.activation(out=c_term[:], in_=spread[:], func=FUNC.Identity, bias=2.0, scale=-0.5)
+
+        dots = {}
+
+        def multiply(chunk):
             dot = dot_psum.tile([P, PAIR * CODES], F32)
             for j in range(PAIR):
                 nc.tensor.matmul_mx(
@@ -143,16 +150,48 @@ def tile_codingclassifier_s_kernel(tc, output, code_book, out):
                     start=True,
                     stop=True,
                 )
+            dots[chunk] = dot
+
+        def finish(chunk):
             result = work.tile([P, PAIR * CODES], F32)
-            nc.vector.scalar_tensor_tensor(
-                out=result[:],
-                in0=dot[:],
-                scalar=2.0 / CODES,
-                in1=both_terms[:, chunk, :],
-                op0=ALU.mult,
-                op1=ALU.add,
-            )
+            for j in range(PAIR):
+                columns = slice(j * CODES, (j + 1) * CODES)
+                nc.vector.scalar_tensor_tensor(
+                    out=result[:, columns],
+                    in0=dots[chunk][:, columns],
+                    scalar=o_term[chunk][:, j : j + 1],
+                    in1=c_term[:],
+                    op0=ALU.add,
+                    op1=ALU.add,
+                )
             nc.sync.dma_start(
                 out=out_view[:, chunk * PAIR : (chunk + 1) * PAIR, :],
                 in_=result[:].rearrange("p (j k) -> p j k", j=PAIR),
             )
+
+        x_transpose(0, split=True)
+        for a in range(CODE_TILES):
+            scale_and_sum_vector(nc, y_rows[a][:], y_scaled[a][:], c_part[a][:], Y_SCALE)
+        transpose(0, [y_scaled[a][:] for a in range(CODE_TILES)], split=True)
+        spread_c_term()
+        sums(0, scale_and_sum_vector)
+        quantise(1)
+        x_transpose(1)
+        sums(1, scale_and_sum_vector, [0])
+        quantise(0)
+        sums(1, scale_and_sum_vector, [1])
+        x_transpose(2)
+        quantise(2)
+        multiply(0)
+        x_transpose(3)
+        finish(0)
+        multiply(1)
+        quantise(3)
+        finish(1)
+        sums_tensor(2)
+        sums(3, scale_and_sum_scalar)
+        multiply(2)
+        quantise(4)
+        finish(2)
+        multiply(3)
+        finish(3)

@@ -72,6 +72,12 @@ def tile_codingclassifier_s_kernel(tc, output, code_book, out):
         for chunk in range(1, CHUNKS):
             load_x(chunk, 1)
 
+        zeros = keep.tile([P, CODES], F32)
+        nc.vector.memset(zeros[:], 0.0)
+        for i in range(2):
+            idle = dot_psum.tile([P, PAIR * CODES], F32, name="dot")
+            nc.tensor.matmul(idle[:, 0:CODES], lhsT=zeros[:, 0:P], rhs=zeros[:], start=True, stop=True)
+
         identity = keep.tile([P, P], F32)
         make_identity(nc, identity[:])
 
@@ -139,7 +145,7 @@ def tile_codingclassifier_s_kernel(tc, output, code_book, out):
         dots = {}
 
         def multiply(chunk):
-            dot = dot_psum.tile([P, PAIR * CODES], F32)
+            dot = dot_psum.tile([P, PAIR * CODES], F32, name="dot")
             for j in range(PAIR):
                 nc.tensor.matmul_mx(
                     out=dot[:, j * CODES : (j + 1) * CODES],

@@ -47,9 +47,8 @@ def tile_codingclassifier_s_kernel(tc, output, code_book, out):
         keep = ctx.enter_context(tc.tile_pool(name="keep", bufs=1))
         work = ctx.enter_context(tc.tile_pool(name="work", bufs=CHUNKS))
         t_psum = ctx.enter_context(tc.psum_pool(name="t_psum", bufs=4))
-        dot_psum = ctx.enter_context(tc.psum_pool(name="dot_psum", bufs=2))
+        dot_psum = ctx.enter_context(tc.psum_pool(name="dot_psum", bufs=3))
         c_psum = ctx.enter_context(tc.psum_pool(name="c_psum", bufs=1))
-        o_psum = ctx.enter_context(tc.psum_pool(name="o_psum", bufs=1))
 
         x_rows = []
         y_rows = []
@@ -88,8 +87,6 @@ def tile_codingclassifier_s_kernel(tc, output, code_book, out):
 
         y_scaled = [keep.tile([P, LENGTH], BF16, name=f"y_scaled{a}") for a in range(CODE_TILES)]
         c_part = [keep.tile([P, 1], F32, name=f"c_part{a}") for a in range(CODE_TILES)]
-        o_scale = keep.tile([P, 1], BF16)
-        nc.vector.memset(o_scale[:], O_SCALE)
         c_term = keep.tile([P, CODES], F32)
         scratch = [keep.tile([P, PAIR, LENGTH], BF16, name=f"scratch{i}") for i in range(CHUNKS)]
         o_term = [keep.tile([P, PAIR], F32, name=f"o_term{i}") for i in range(CHUNKS)]
@@ -122,16 +119,6 @@ def tile_codingclassifier_s_kernel(tc, output, code_book, out):
                 scale_and_sum(
                     nc, x_rows[chunk][j], scratch[chunk][:, j, :], o_term[chunk][:, j : j + 1], O_SCALE
                 )
-
-        def sums_tensor(chunk):
-            total = o_psum.tile([P, PAIR], F32)
-            values = grouped[:, 1 + chunk, :].rearrange("p (j n t) -> p j n t", j=PAIR, t=4)
-            for j in range(PAIR):
-                for t in range(4):
-                    nc.tensor.matmul(
-                        total[:, j : j + 1], lhsT=values[:, j, :, t], rhs=o_scale[:], start=(t == 0), stop=(t == 3)
-                    )
-            o_term[chunk] = total
 
         def x_transpose(chunk, split=False):
             transpose(1 + chunk, x_rows[chunk], split)
@@ -187,14 +174,14 @@ def tile_codingclassifier_s_kernel(tc, output, code_book, out):
         quantise(0)
         sums(1, scale_and_sum_vector, [1])
         x_transpose(2)
-        quantise(2)
-        multiply(0)
         x_transpose(3)
+        multiply(0)
+        sums(2, scale_and_sum_vector)
+        quantise(2)
         finish(0)
         multiply(1)
         quantise(3)
         finish(1)
-        sums_tensor(2)
         sums(3, scale_and_sum_scalar)
         multiply(2)
         quantise(4)

@@ -19,6 +19,8 @@ WORDS = LENGTH // 2
 ROW_TILES = ROWS // P
 CODE_TILES = CODES // P
 PAIR = 2
+WARM_COLUMNS = 240
+BANK = 512
 CHUNKS = ROW_TILES // PAIR
 
 Y_SCALE = 2.0 / CODES
@@ -46,9 +48,11 @@ def tile_codingclassifier_s_kernel(tc, output, code_book, out):
         ctx.enter_context(tc.manual_schedule())
         keep = ctx.enter_context(tc.tile_pool(name="keep", bufs=1))
         work = ctx.enter_context(tc.tile_pool(name="work", bufs=CHUNKS))
-        t_psum = ctx.enter_context(tc.psum_pool(name="t_psum", bufs=4))
-        dot_psum = ctx.enter_context(tc.psum_pool(name="dot_psum", bufs=3))
-        c_psum = ctx.enter_context(tc.psum_pool(name="c_psum", bufs=1))
+        psum = ctx.enter_context(tc.psum_pool(name="psum", bufs=8))
+
+        def new_bank():
+            return psum.tile([P, BANK], F32, name="bank")
+
 
         x_rows = []
         y_rows = []
@@ -63,32 +67,38 @@ def tile_codingclassifier_s_kernel(tc, output, code_book, out):
                 tiles.extend(x_piece[:, j, :] for j in range(span))
             x_rows.append(tiles)
 
-        load_x(0, PAIR)
         for a in range(CODE_TILES):
             y_tile = keep.tile([P, LENGTH], BF16, name=f"y_tile{a}")
             nc.sync.dma_start(out=y_tile[:], in_=code_book[a * P : (a + 1) * P, :])
             y_rows.append(y_tile)
+        load_x(0, PAIR)
         for chunk in range(1, CHUNKS):
             load_x(chunk, 1)
 
-        zeros = keep.tile([P, CODES], F32)
+        zeros = keep.tile([P, 1], F32)
         nc.vector.memset(zeros[:], 0.0)
         for i in range(2):
-            idle = dot_psum.tile([P, PAIR * CODES], F32, name="dot")
-            nc.tensor.matmul(idle[:, 0:CODES], lhsT=zeros[:, 0:P], rhs=zeros[:], start=True, stop=True)
+            idle = new_bank()
+            nc.tensor.matmul(
+                idle[:, 0:WARM_COLUMNS],
+                lhsT=zeros[:].to_broadcast([P, P]),
+                rhs=zeros[:].to_broadcast([P, WARM_COLUMNS]),
+                start=True,
+                stop=True,
+            )
 
         identity = keep.tile([P, P], F32)
         make_identity(nc, identity[:])
 
-        warm = keep.tile([P, 1], F32)
-        nc.vector.memset(warm[:], 0.0)
         warmed = keep.tile([P, 1], F32)
-        nc.scalar.activation(out=warmed[:], in_=warm[:], func=FUNC.Identity)
+        nc.scalar.activation(out=warmed[:], in_=zeros[:], func=FUNC.Identity)
 
         y_scaled = [keep.tile([P, LENGTH], BF16, name=f"y_scaled{a}") for a in range(CODE_TILES)]
         c_part = [keep.tile([P, 1], F32, name=f"c_part{a}") for a in range(CODE_TILES)]
         c_term = keep.tile([P, CODES], F32)
         scratch = [keep.tile([P, PAIR, LENGTH], BF16, name=f"scratch{i}") for i in range(CHUNKS)]
+        o_scale = keep.tile([P, 1], BF16)
+        nc.vector.memset(o_scale[:], O_SCALE)
         o_term = [keep.tile([P, PAIR], F32, name=f"o_term{i}") for i in range(CHUNKS)]
 
         grouped = keep.tile([P, 1 + CHUNKS, PAIR * P * 4], BF16, align_bytes=64)
@@ -99,7 +109,7 @@ def tile_codingclassifier_s_kernel(tc, output, code_book, out):
             packed = grouped[:, i, :].bitcast(F32).rearrange("p (j n u) -> p j n u", j=PAIR, u=2)
             span = 1 if split else PAIR
             for first in range(0, PAIR, span):
-                bank = t_psum.tile([P, PAIR, 2, P], F32)
+                bank = new_bank()[:].rearrange("p (j u n) -> p j u n", j=PAIR, u=2)
                 for j in range(span):
                     words = tiles[first + j].bitcast(F32)
                     for u in range(2):
@@ -114,28 +124,44 @@ def tile_codingclassifier_s_kernel(tc, output, code_book, out):
                 out=codes[:, i, :].bitcast(FP8X4), scales=scales[:, i, :], in_=grouped[:, i, :]
             )
 
-        def sums(chunk, scale_and_sum, tiles=range(PAIR)):
-            for j in tiles:
-                scale_and_sum(
-                    nc, x_rows[chunk][j], scratch[chunk][:, j, :], o_term[chunk][:, j : j + 1], O_SCALE
-                )
+        def sums_vector(chunk, j):
+            scale_and_sum_vector(
+                nc, x_rows[chunk][j], scratch[chunk][:, j, :], o_term[chunk][:, j : j + 1], O_SCALE
+            )
 
         def x_transpose(chunk, split=False):
             transpose(1 + chunk, x_rows[chunk], split)
 
         def spread_c_term():
-            spread = c_psum.tile([P, CODES], F32)
-            nc.tensor.transpose(spread[:, 0:P], c_part[0][:].to_broadcast([P, P]), identity[:])
-            nc.tensor.transpose(spread[:, P:CODES], c_part[1][:].to_broadcast([P, P]), identity[:])
-            nc.scalar.activation(out=c_term[:], in_=spread[:], func=FUNC.Identity, bias=2.0, scale=-0.5)
+            spread = new_bank()
+            for a in range(CODE_TILES):
+                nc.tensor.transpose(
+                    spread[:, a * P : (a + 1) * P], c_part[a][:].to_broadcast([P, P]), identity[:]
+                )
+            return spread
+
+        def finish_c_term(spread):
+            nc.vector.tensor_scalar(
+                out=c_term[:], in0=spread[:, 0:CODES], scalar1=-0.5, scalar2=2.0, op0=ALU.mult, op1=ALU.add
+            )
 
         dots = {}
 
-        def multiply(chunk):
-            dot = dot_psum.tile([P, PAIR * CODES], F32, name="dot")
+        def sums_tensor(chunk):
+            values = grouped[:, 1 + chunk, :].rearrange("p (j n t) -> p j n t", j=PAIR, t=4)
+            total = new_bank()
             for j in range(PAIR):
+                for t in range(4):
+                    nc.tensor.matmul(
+                        total[:, j : j + 1], lhsT=values[:, j, :, t], rhs=o_scale[:], start=(t == 0), stop=(t == 3)
+                    )
+            o_term[chunk] = total
+
+        def multiply(chunk):
+            for j in range(PAIR):
+                dot = new_bank()
                 nc.tensor.matmul_mx(
-                    out=dot[:, j * CODES : (j + 1) * CODES],
+                    out=dot[:, 0:CODES],
                     lhsT=codes[:, 1 + chunk, j * P : (j + 1) * P].bitcast(FP8X4),
                     lhsT_scale=scales[:, 1 + chunk, j * P : (j + 1) * P],
                     rhs=codes[:, 0, :].bitcast(FP8X4),
@@ -143,48 +169,55 @@ def tile_codingclassifier_s_kernel(tc, output, code_book, out):
                     start=True,
                     stop=True,
                 )
-            dots[chunk] = dot
+                dots[chunk, j] = dot
+
+        results = [keep.tile([P, PAIR, CODES], F32, name=f"result{i}") for i in range(CHUNKS)]
 
         def finish(chunk):
-            result = work.tile([P, PAIR * CODES], F32)
             for j in range(PAIR):
-                columns = slice(j * CODES, (j + 1) * CODES)
                 nc.vector.scalar_tensor_tensor(
-                    out=result[:, columns],
-                    in0=dots[chunk][:, columns],
+                    out=results[chunk][:, j, :],
+                    in0=dots[chunk, j][:, 0:CODES],
                     scalar=o_term[chunk][:, j : j + 1],
                     in1=c_term[:],
                     op0=ALU.add,
                     op1=ALU.add,
                 )
-            nc.sync.dma_start(
-                out=out_view[:, chunk * PAIR : (chunk + 1) * PAIR, :],
-                in_=result[:].rearrange("p (j k) -> p j k", j=PAIR),
-            )
+                if chunk == CHUNKS - 1:
+                    store(chunk, j, j + 1)
 
-        x_transpose(0, split=True)
+        def store(chunk, first, last):
+            r = chunk * PAIR
+            nc.sync.dma_start(out=out_view[:, r + first : r + last, :], in_=results[chunk][:, first:last, :])
+
         for a in range(CODE_TILES):
             scale_and_sum_vector(nc, y_rows[a][:], y_scaled[a][:], c_part[a][:], Y_SCALE)
         transpose(0, [y_scaled[a][:] for a in range(CODE_TILES)], split=True)
-        spread_c_term()
-        sums(0, scale_and_sum_vector)
-        quantise(1)
+        spread = spread_c_term()
+        sums_vector(0, 0)
+        sums_vector(0, 1)
+        x_transpose(0, split=True)
+        sums_vector(1, 0)
+        finish_c_term(spread)
         x_transpose(1)
-        sums(1, scale_and_sum_vector, [0])
         quantise(0)
-        sums(1, scale_and_sum_vector, [1])
         x_transpose(2)
+        sums_vector(1, 1)
+        quantise(1)
         x_transpose(3)
         multiply(0)
-        sums(2, scale_and_sum_vector)
         quantise(2)
-        finish(0)
         multiply(1)
+        sums_tensor(2)
+        finish(0)
+        store(0, 0, 2)
         quantise(3)
-        finish(1)
-        sums(3, scale_and_sum_scalar)
         multiply(2)
+        sums_tensor(3)
+        finish(1)
+        store(1, 0, 2)
         quantise(4)
-        finish(2)
         multiply(3)
+        finish(2)
+        store(2, 0, 2)
         finish(3)

from contextlib import ExitStack

import concourse.mybir as mybir
from concourse.masks import make_identity

F32 = mybir.dt.float32
BF16 = mybir.dt.bfloat16
U32 = mybir.dt.uint32
U8 = mybir.dt.uint8
FP8X4 = mybir.dt.float8_e4m3fn_x4
ALU = mybir.AluOpType
FUNC = mybir.ActivationFunctionType

P = 128
ROWS = 1024
CODES = 256
LENGTH = 512
WORDS = LENGTH // 2
ROW_TILES = ROWS // P
CODE_TILES = CODES // P
PAIR = 2
WARM_COLUMNS = 240
BANK = 512
CHUNKS = ROW_TILES // PAIR

Y_SCALE = 2.0 / CODES
O_SCALE = -1.0 / CODES

FLOPS = 2 * ROWS * CODES * LENGTH


def scale_and_sum_vector(nc, rows, scaled, total, factor):
    nc.vector.tensor_scalar(
        out=scaled, in0=rows, scalar1=factor, scalar2=None, op0=ALU.mult, op1=ALU.add, accum_out=total
    )


def scale_and_sum_scalar(nc, rows, scaled, total, factor):
    nc.scalar.activation(out=scaled, in_=rows, func=FUNC.Identity, scale=factor, accum_out=total)


def tile_codingclassifier_s_kernel(tc, output, code_book, out):
    nc = tc.nc
    x_view = output.rearrange("(p r) c -> p r c", r=ROW_TILES)
    out_view = out.rearrange("(p r) k -> p r k", r=ROW_TILES)

    with ExitStack() as ctx:
        ctx.enter_context(tc.manual_schedule())
        keep = ctx.enter_context(tc.tile_pool(name="keep", bufs=1))
        work = ctx.enter_context(tc.tile_pool(name="work", bufs=CHUNKS))
        psum = ctx.enter_context(tc.psum_pool(name="psum", bufs=8))

        def new_bank():
            return psum.tile([P, BANK], F32, name="bank")


        x_rows = []
        y_rows = []

        def load_x(chunk, pieces):
            tiles = []
            for piece in range(pieces):
                span = PAIR // pieces
                first = chunk * PAIR + piece * span
                x_piece = keep.tile([P, span, LENGTH], BF16, name=f"x{chunk}_{piece}")
                nc.sync.dma_start(out=x_piece[:], in_=x_view[:, first : first + span, :])
                tiles.extend(x_piece[:, j, :] for j in range(span))
            x_rows.append(tiles)

        for a in range(CODE_TILES):
            y_tile = keep.tile([P, LENGTH], BF16, name=f"y_tile{a}")
            nc.sync.dma_start(out=y_tile[:], in_=code_book[a * P : (a + 1) * P, :])
            y_rows.append(y_tile)
        load_x(0, PAIR)
        for chunk in range(1, CHUNKS):
            load_x(chunk, 1)

        zeros = keep.tile([P, 1], F32)
        nc.vector.memset(zeros[:], 0.0)
        for i in range(2):
            idle = new_bank()
            nc.tensor.matmul(
                idle[:, 0:WARM_COLUMNS],
                lhsT=zeros[:].to_broadcast([P, P]),
                rhs=zeros[:].to_broadcast([P, WARM_COLUMNS]),
                start=True,
                stop=True,
            )

        identity = keep.tile([P, P], F32)
        make_identity(nc, identity[:])

        warmed = keep.tile([P, 1], F32)
        nc.scalar.activation(out=warmed[:], in_=zeros[:], func=FUNC.Identity)

        y_scaled = [keep.tile([P, LENGTH], BF16, name=f"y_scaled{a}") for a in range(CODE_TILES)]
        c_part = [keep.tile([P, 1], F32, name=f"c_part{a}") for a in range(CODE_TILES)]
        c_term = keep.tile([P, CODES], F32)
        scratch = [keep.tile([P, PAIR, LENGTH], BF16, name=f"scratch{i}") for i in range(CHUNKS)]
        o_scale = keep.tile([P, 1], BF16)
        nc.vector.memset(o_scale[:], O_SCALE)
        o_term = [keep.tile([P, PAIR], F32, name=f"o_term{i}") for i in range(CHUNKS)]

        grouped = keep.tile([P, 1 + CHUNKS, PAIR * P * 4], BF16, align_bytes=64)
        codes = keep.tile([P, 1 + CHUNKS, PAIR * P], U32, align_bytes=64)
        scales = keep.tile([P, 1 + CHUNKS, PAIR * P], U8, align_bytes=64)

        def transpose(i, tiles, split):
            packed = grouped[:, i, :].bitcast(F32).rearrange("p (j n u) -> p j n u", j=PAIR, u=2)
            span = 1 if split else PAIR
            for first in range(0, PAIR, span):
                bank = new_bank()[:].rearrange("p (j u n) -> p j u n", j=PAIR, u=2)
                for j in range(span):
                    words = tiles[first + j].bitcast(F32)
                    for u in range(2):
                        nc.tensor.transpose(bank[:, j, u, :], words[:, u:WORDS:2], identity[:])
                nc.scalar.copy(
                    out=packed[:, first : first + span, :, :],
                    in_=bank[:, 0:span, :, :].rearrange("p j u n -> p j n u"),
                )

        def quantise(i):
            nc.vector.quantize_mx(
                out=codes[:, i, :].bitcast(FP8X4), scales=scales[:, i, :], in_=grouped[:, i, :]
            )

        def sums_vector(chunk, j):
            scale_and_sum_vector(
                nc, x_rows[chunk][j], scratch[chunk][:, j, :], o_term[chunk][:, j : j + 1], O_SCALE
            )

        def x_transpose(chunk, split=False):
            transpose(1 + chunk, x_rows[chunk], split)

        def spread_c_term():
            spread = new_bank()
            for a in range(CODE_TILES):
                nc.tensor.transpose(
                    spread[:, a * P : (a + 1) * P], c_part[a][:].to_broadcast([P, P]), identity[:]
                )
            return spread

        def finish_c_term(spread):
            nc.vector.tensor_scalar(
                out=c_term[:], in0=spread[:, 0:CODES], scalar1=-0.5, scalar2=2.0, op0=ALU.mult, op1=ALU.add
            )

        dots = {}

        def sums_tensor(chunk):
            values = grouped[:, 1 + chunk, :].rearrange("p (j n t) -> p j n t", j=PAIR, t=4)
            total = new_bank()
            for j in range(PAIR):
                for t in range(4):
                    nc.tensor.matmul(
                        total[:, j : j + 1], lhsT=values[:, j, :, t], rhs=o_scale[:], start=(t == 0), stop=(t == 3)
                    )
            o_term[chunk] = total

        def multiply(chunk):
            for j in range(PAIR):
                dot = new_bank()
                nc.tensor.matmul_mx(
                    out=dot[:, 0:CODES],
                    lhsT=codes[:, 1 + chunk, j * P : (j + 1) * P].bitcast(FP8X4),
                    lhsT_scale=scales[:, 1 + chunk, j * P : (j + 1) * P],
                    rhs=codes[:, 0, :].bitcast(FP8X4),
                    rhs_scale=scales[:, 0, :],
                    start=True,
                    stop=True,
                )
                dots[chunk, j] = dot

        results = [keep.tile([P, PAIR, CODES], F32, name=f"result{i}") for i in range(CHUNKS)]

        def finish(chunk):
            for j in range(PAIR):
                nc.vector.scalar_tensor_tensor(
                    out=results[chunk][:, j, :],
                    in0=dots[chunk, j][:, 0:CODES],
                    scalar=o_term[chunk][:, j : j + 1],
                    in1=c_term[:],
                    op0=ALU.add,
                    op1=ALU.add,
                )
                if chunk == CHUNKS - 1:
                    store(chunk, j, j + 1)

        def store(chunk, first, last):
            r = chunk * PAIR
            nc.sync.dma_start(out=out_view[:, r + first : r + last, :], in_=results[chunk][:, first:last, :])

        for a in range(CODE_TILES):
            scale_and_sum_vector(nc, y_rows[a][:], y_scaled[a][:], c_part[a][:], Y_SCALE)
        transpose(0, [y_scaled[a][:] for a in range(CODE_TILES)], split=True)
        spread = spread_c_term()
        sums_vector(0, 0)
        sums_vector(0, 1)
        x_transpose(0, split=True)
        sums_vector(1, 0)
        finish_c_term(spread)
        x_transpose(1)
        quantise(0)
        x_transpose(2)
        sums_vector(1, 1)
        quantise(1)
        x_transpose(3)
        multiply(0)
        quantise(2)
        multiply(1)
        sums_tensor(2)
        finish(0)
        store(0, 0, 2)
        quantise(3)
        multiply(2)
        sums_tensor(3)
        finish(1)
        store(1, 0, 2)
        quantise(4)
        multiply(3)
        finish(2)
        store(2, 0, 2)
        finish(3)
